import numpy as np
import ml_dtypes


def mxq(x, axis, fmt="e4m3"):
    dtype, down = {"e4m3": (ml_dtypes.float8_e4m3fn, 7), "e5m2": (ml_dtypes.float8_e5m2, 14)}[fmt]
    v = np.moveaxis(np.asarray(x, np.float32).astype(ml_dtypes.bfloat16).astype(np.float64), axis, -1)
    blocks = v.reshape(v.shape[:-1] + (-1, 32))
    amax = np.abs(blocks).max(-1, keepdims=True)
    byte = np.maximum(np.where(amax > 0, np.frexp(amax)[1] - 1 + 127, 0) - down, 1)
    scale = np.exp2(byte - 127.0)
    codes = (blocks / scale).astype(np.float32).astype(dtype).astype(np.float64)
    return np.moveaxis((codes * scale).reshape(v.shape), -1, axis)


WIDE = False


def mx_kscale(k):
    if not WIDE:
        return np.ones(k)
    levels = np.array([10, -10, 5, -5, 0])
    a = np.random.permutation(np.resize(levels, k // 512 * 4)).reshape(k // 512, 4)
    idx = np.arange(k)
    return np.exp2(a[idx // 512, idx % 128 // 32])


BF16 = ml_dtypes.bfloat16


def bf(x):
    return np.asarray(x, np.float32).astype(BF16)


def f64(x):
    return np.asarray(x).astype(np.float64)


B, N, W, H, D = 2, 16, 512, 2, 128


def setup_inputs():
    s = mx_kscale(W)[:, None]
    m = np.random.uniform(0.2, 1.0, (N, N))
    return {"k_feat": bf(np.maximum(np.random.standard_normal((B, H, N, W, D)) * 0.5, 0.0) * s),
            "v": bf(np.random.standard_normal((B, H, N, W, D)) * 0.5 / s),
            "w_piece": bf(m / m.sum(axis=0, keepdims=True))}


def reference(k_feat, v, w_piece):
    kq = mxq(f64(k_feat), 3, "e4m3")
    vq = mxq(f64(v), 3, "e4m3")
    kv = kq.transpose(0, 1, 2, 4, 3) @ vq
    wp = f64(w_piece)
    return (wp[None, None, :, :, None, None] * kv[:, :, None, :, :, :]).sum(axis=3)

@@ -1,0 +1,170 @@
+import concourse.mybir as mybir
+from concourse.masks import make_identity
+
+F32 = mybir.dt.float32
+BF16 = mybir.dt.bfloat16
+U32 = mybir.dt.uint32
+U8 = mybir.dt.uint8
+FP8X4 = mybir.dt.float8_e4m3fn_x4
+MULT = mybir.AluOpType.mult
+ADD = mybir.AluOpType.add
+AXIS_X = mybir.AxisListType.X
+
+P = 128
+PACK = 4
+GROUPS = 4
+WINDOWS = 16
+HEAD = 128
+RUN = 4
+LANES = P // WINDOWS
+TENSOR_SLABS = 6
+TENSOR_COLS = TENSOR_SLABS * LANES
+VECTOR_COLS = HEAD - TENSOR_COLS
+LOADS_AHEAD = 6
+LAST = 4
+
+FLOPS = 2 * GROUPS * WINDOWS * (P * PACK) * HEAD * HEAD + 2 * GROUPS * WINDOWS * WINDOWS * HEAD * HEAD
+
+
+def tile_mhla_pa_t_kernel(tc, k_feat, v, w_piece, out):
+    nc = tc.nc
+    dram_rows = {
+        "k": k_feat.rearrange("b h n (p t) d -> n p (b h) (t d)", t=PACK),
+        "v": v.rearrange("b h n (p t) d -> n p (b h) (t d)", t=PACK),
+    }
+    out_rows = out.rearrange("b h i d e -> i d (b h) e")
+
+    with tc.tile_pool(name="keep", bufs=1) as keep, tc.tile_pool(name="raw", bufs=LOADS_AHEAD) as raw_pool, tc.tile_pool(
+        name="stage", bufs=3
+    ) as stage, tc.tile_pool(name="turn", bufs=2) as turn, tc.psum_pool(name="psum", bufs=2) as psum:
+        raw = {}
+
+        def load(j):
+            for name in ("k", "v"):
+                t = raw_pool.tile([P, GROUPS, PACK, HEAD], BF16, name="raw_" + name)
+                nc.sync.dma_start(out=t[:].rearrange("p g t d -> p g (t d)"), in_=dram_rows[name][j])
+                raw[(name, j)] = t
+
+        w_bf = keep.tile([P, WINDOWS * WINDOWS], BF16)
+        nc.scalar.dma_start(out=w_bf[:], in_=w_piece.rearrange("i j -> (i j)").partition_broadcast(P))
+        for j in range(LOADS_AHEAD):
+            load(j)
+
+        w_all = keep.tile([P, WINDOWS, WINDOWS], F32)
+        nc.vector.tensor_copy(out=w_all[:].rearrange("p i j -> p (i j)"), in_=w_bf[:])
+        ident = keep.tile([P, P], F32)
+        make_identity(nc, ident[:])
+        own_j = keep.tile([P, WINDOWS], F32)
+        nc.vector.tensor_reduce(out=own_j[:], in_=ident[:].rearrange("p (j x) -> p j x", x=LANES), axis=AXIS_X, op=ADD)
+        own_x = keep.tile([P, LANES], F32)
+        nc.vector.tensor_reduce(out=own_x[:], in_=ident[:].rearrange("p (j x) -> p x j", x=LANES), axis=AXIS_X, op=ADD)
+        picked = keep.tile([P, WINDOWS, WINDOWS], F32)
+        nc.vector.tensor_tensor(
+            out=picked[:], in0=w_all[:], in1=own_j[:].unsqueeze(1).to_broadcast([P, WINDOWS, WINDOWS]), op=MULT
+        )
+        w_row = keep.tile([P, WINDOWS], F32)
+        nc.vector.tensor_reduce(out=w_row[:], in_=picked[:], axis=AXIS_X, op=ADD)
+        w_kron = keep.tile([P, WINDOWS, LANES], F32)
+        nc.vector.tensor_tensor(
+            out=w_kron[:],
+            in0=w_row[:].unsqueeze(2).to_broadcast([P, WINDOWS, LANES]),
+            in1=own_x[:].unsqueeze(1).to_broadcast([P, WINDOWS, LANES]),
+            op=MULT,
+        )
+
+        kv_tensor = keep.tile([P, GROUPS, TENSOR_SLABS, WINDOWS, LANES], F32)
+        kv_vector = keep.tile([P, WINDOWS, GROUPS, VECTOR_COLS], F32)
+        out_sb = keep.tile([P, WINDOWS, GROUPS, HEAD], F32)
+
+        def regroup(j):
+            grouped = {}
+            for name in ("k", "v"):
+                dst = stage.tile([P, GROUPS * HEAD, PACK], BF16, name="grouped_" + name, align_bytes=64)
+                for g in range(GROUPS):
+                    dst_g = dst[:, g * HEAD : (g + 1) * HEAD, :].rearrange("p (c i) t -> p c t i", i=RUN)
+                    src_g = raw[(name, j)][:, g, :, :].rearrange("p t (c i) -> p c t i", i=RUN)
+                    if j == 0:
+                        nc.vector.tensor_copy(out=dst_g, in_=src_g)
+                    else:
+                        nc.scalar.copy(out=dst_g, in_=src_g)
+                grouped[name] = dst
+            return grouped
+
+        def states(grouped, j):
+            codes = {}
+            scales = {}
+            for name in ("k", "v"):
+                codes[name] = stage.tile([P, GROUPS * HEAD], U32, name="codes_" + name, align_bytes=64)
+                scales[name] = stage.tile([P, GROUPS * HEAD], U8, name="scales_" + name, align_bytes=64)
+                nc.vector.quantize_mx(
+                    out=codes[name][:].bitcast(FP8X4),
+                    scales=scales[name][:],
+                    in_=grouped[name][:].rearrange("p c t -> p (c t)"),
+                )
+            kv_ps = psum.tile([P, GROUPS, HEAD], F32)
+            for g in range(GROUPS):
+                cols = slice(g * HEAD, (g + 1) * HEAD)
+                nc.tensor.matmul_mx(
+                    out=kv_ps[:, g, :],
+                    lhsT=codes["k"][:, cols].bitcast(FP8X4),
+                    lhsT_scale=scales["k"][:, cols],
+                    rhs=codes["v"][:, cols].bitcast(FP8X4),
+                    rhs_scale=scales["v"][:, cols],
+                    start=True,
+                    stop=True,
+                )
+            nc.scalar.copy(
+                out=kv_tensor[:, :, :, j, :],
+                in_=kv_ps[:, :, 0:TENSOR_COLS].rearrange("p g (c x) -> p g c x", x=LANES),
+            )
+            nc.scalar.copy(out=kv_vector[:, j, :, :], in_=kv_ps[:, :, TENSOR_COLS:HEAD])
+
+        def vector_mix(i, j):
+            acc = out_sb[:, i, :, TENSOR_COLS:HEAD]
+            if j == 0:
+                nc.vector.tensor_scalar_mul(out=acc, in0=kv_vector[:, j, :, :], scalar1=w_all[:, i, j : j + 1])
+            else:
+                nc.vector.scalar_tensor_tensor(
+                    out=acc, in0=kv_vector[:, j, :, :], scalar=w_all[:, i, j : j + 1], in1=acc, op0=MULT, op1=ADD
+                )
+
+        def tensor_mix(c):
+            tr_ps = psum.tile([P, GROUPS, HEAD], F32)
+            for g in range(GROUPS):
+                nc.tensor.transpose(
+                    out=tr_ps[:, g, :], in_=kv_tensor[:, g, c, :, :].rearrange("p j x -> p (j x)"), identity=ident[:]
+                )
+            kvt_sb = turn.tile([P, GROUPS, HEAD], F32)
+            nc.scalar.copy(out=kvt_sb[:], in_=tr_ps[:])
+            mix_ps = psum.tile([P, GROUPS, HEAD], F32)
+            for g in range(GROUPS):
+                nc.tensor.matmul(
+                    out=mix_ps[:, g, :],
+                    lhsT=kvt_sb[:, g, :],
+                    rhs=w_kron[:].rearrange("p i y -> p (i y)"),
+                    start=True,
+                    stop=True,
+                )
+            nc.scalar.copy(
+                out=out_sb[:, :, :, c * LANES : (c + 1) * LANES],
+                in_=mix_ps[:].rearrange("p g (i y) -> p i g y", y=LANES),
+            )
+
+        grouped = regroup(0)
+        for j in range(WINDOWS):
+            following = None
+            if j + 1 < WINDOWS:
+                following = regroup(j + 1)
+            if j + LOADS_AHEAD < WINDOWS:
+                load(j + LOADS_AHEAD)
+            states(grouped, j)
+            if j < WINDOWS - LAST:
+                for i in range(WINDOWS):
+                    vector_mix(i, j)
+            grouped = following
+        for c in range(TENSOR_SLABS):
+            tensor_mix(c)
+        for i in range(WINDOWS):
+            for j in range(WINDOWS - LAST, WINDOWS):
+                vector_mix(i, j)
+            nc.sync.dma_start(out=out_rows[i], in_=out_sb[:, i, :, :])

@@ -21,6 +21,7 @@ TENSOR_SLABS = 6
 TENSOR_COLS = TENSOR_SLABS * LANES
 VECTOR_COLS = HEAD - TENSOR_COLS
 LOADS_AHEAD = 6
+CHAINS = 2
 LAST = 4
 
 FLOPS = 2 * GROUPS * WINDOWS * (P * PACK) * HEAD * HEAD + 2 * GROUPS * WINDOWS * WINDOWS * HEAD * HEAD
@@ -164,7 +165,9 @@ def tile_mhla_pa_t_kernel(tc, k_feat, v, w_piece, out):
             grouped = following
         for c in range(TENSOR_SLABS):
             tensor_mix(c)
-        for i in range(WINDOWS):
+        for first in range(0, WINDOWS, CHAINS):
             for j in range(WINDOWS - LAST, WINDOWS):
-                vector_mix(i, j)
-            nc.sync.dma_start(out=out_rows[i], in_=out_sb[:, i, :, :])
+                for i in range(first, first + CHAINS):
+                    vector_mix(i, j)
+            for i in range(first, first + CHAINS):
+                nc.sync.dma_start(out=out_rows[i], in_=out_sb[:, i, :, :])

@@ -18,8 +18,9 @@ HEAD = 128
 RUN = 4
 LANES = P // WINDOWS
 TENSOR_SLABS = 6
+HALF = HEAD // 2
 TENSOR_COLS = TENSOR_SLABS * LANES
-VECTOR_COLS = HEAD - TENSOR_COLS
+GPSIMD_COLS = HALF - TENSOR_COLS
 LOADS_AHEAD = 6
 CHAINS = 2
 LAST = 4
@@ -37,7 +38,7 @@ def tile_mhla_pa_t_kernel(tc, k_feat, v, w_piece, out):
 
     with tc.tile_pool(name="keep", bufs=1) as keep, tc.tile_pool(name="raw", bufs=LOADS_AHEAD) as raw_pool, tc.tile_pool(
         name="stage", bufs=3
-    ) as stage, tc.tile_pool(name="turn", bufs=2) as turn, tc.psum_pool(name="psum", bufs=2) as psum:
+    ) as stage, tc.tile_pool(name="turn", bufs=2) as turn, tc.psum_pool(name="psum_v", bufs=LAST) as psum_v:
         raw = {}
 
         def load(j):
@@ -74,7 +75,8 @@ def tile_mhla_pa_t_kernel(tc, k_feat, v, w_piece, out):
         )
 
         kv_tensor = keep.tile([P, GROUPS, TENSOR_SLABS, WINDOWS, LANES], F32)
-        kv_vector = keep.tile([P, WINDOWS, GROUPS, VECTOR_COLS], F32)
+        kv_gpsimd = keep.tile([P, WINDOWS, GROUPS, GPSIMD_COLS], F32)
+        kv_vector = {}
         out_sb = keep.tile([P, WINDOWS, GROUPS, HEAD], F32)
 
         def regroup(j):
@@ -91,7 +93,7 @@ def tile_mhla_pa_t_kernel(tc, k_feat, v, w_piece, out):
                 grouped[name] = dst
             return grouped
 
-        def states(grouped, j):
+        def states(psum_s, grouped, j):
             codes = {}
             scales = {}
             for name in ("k", "v"):
@@ -102,42 +104,61 @@ def tile_mhla_pa_t_kernel(tc, k_feat, v, w_piece, out):
                     scales=scales[name][:],
                     in_=grouped[name][:].rearrange("p c t -> p (c t)"),
                 )
-            kv_ps = psum.tile([P, GROUPS, HEAD], F32)
-            for g in range(GROUPS):
-                cols = slice(g * HEAD, (g + 1) * HEAD)
-                nc.tensor.matmul_mx(
-                    out=kv_ps[:, g, :],
-                    lhsT=codes["k"][:, cols].bitcast(FP8X4),
-                    lhsT_scale=scales["k"][:, cols],
-                    rhs=codes["v"][:, cols].bitcast(FP8X4),
-                    rhs_scale=scales["v"][:, cols],
-                    start=True,
-                    stop=True,
-                )
+            low_ps = psum_s.tile([P, GROUPS, HALF], F32)
+            high_ps = psum_v.tile([P, GROUPS, HALF], F32)
+            for half, kv_ps in ((0, low_ps), (1, high_ps)):
+                for g in range(GROUPS):
+                    k_cols = slice(g * HEAD, (g + 1) * HEAD)
+                    v_cols = slice(g * HEAD + half * HALF, g * HEAD + (half + 1) * HALF)
+                    nc.tensor.matmul_mx(
+                        out=kv_ps[:, g, :],
+                        lhsT=codes["k"][:, k_cols].bitcast(FP8X4),
+                        lhsT_scale=scales["k"][:, k_cols],
+                        rhs=codes["v"][:, v_cols].bitcast(FP8X4),
+                        rhs_scale=scales["v"][:, v_cols],
+                        start=True,
+                        stop=True,
+                    )
             nc.scalar.copy(
                 out=kv_tensor[:, :, :, j, :],
-                in_=kv_ps[:, :, 0:TENSOR_COLS].rearrange("p g (c x) -> p g c x", x=LANES),
+                in_=low_ps[:, :, 0:TENSOR_COLS].rearrange("p g (c x) -> p g c x", x=LANES),
             )
-            nc.scalar.copy(out=kv_vector[:, j, :, :], in_=kv_ps[:, :, TENSOR_COLS:HEAD])
+            nc.scalar.copy(out=kv_gpsimd[:, j, :, :], in_=low_ps[:, :, TENSOR_COLS:HALF])
+            kv_vector[j] = high_ps
+
+        def gpsimd_mix(j):
+            acc = out_sb[:, :, :, TENSOR_COLS:HALF]
+            shape = [P, WINDOWS, GROUPS, GPSIMD_COLS]
+            state = kv_gpsimd[:, j, :, :].unsqueeze(1).to_broadcast(shape)
+            weight = w_all[:, :, j : j + 1].unsqueeze(3).to_broadcast(shape)
+            if j == 0:
+                nc.gpsimd.tensor_tensor(out=acc, in0=state, in1=weight, op=MULT)
+            else:
+                product = turn.tile(shape, F32)
+                nc.gpsimd.tensor_tensor(out=product[:], in0=state, in1=weight, op=MULT)
+                nc.gpsimd.tensor_tensor(out=acc, in0=acc, in1=product[:], op=ADD)
 
         def vector_mix(i, j):
-            acc = out_sb[:, i, :, TENSOR_COLS:HEAD]
+            acc = out_sb[:, i, :, HALF:HEAD]
             if j == 0:
-                nc.vector.tensor_scalar_mul(out=acc, in0=kv_vector[:, j, :, :], scalar1=w_all[:, i, j : j + 1])
+                nc.vector.tensor_scalar_mul(out=acc, in0=kv_vector[j][:], scalar1=w_all[:, i, j : j + 1])
             else:
                 nc.vector.scalar_tensor_tensor(
-                    out=acc, in0=kv_vector[:, j, :, :], scalar=w_all[:, i, j : j + 1], in1=acc, op0=MULT, op1=ADD
+                    out=acc, in0=kv_vector[j][:], scalar=w_all[:, i, j : j + 1], in1=acc, op0=MULT, op1=ADD
                 )
 
-        def tensor_mix(c):
-            tr_ps = psum.tile([P, GROUPS, HEAD], F32)
+        def turn_slab(psum_t, c):
+            tr_ps = psum_t.tile([P, GROUPS, HEAD], F32)
             for g in range(GROUPS):
                 nc.tensor.transpose(
                     out=tr_ps[:, g, :], in_=kv_tensor[:, g, c, :, :].rearrange("p j x -> p (j x)"), identity=ident[:]
                 )
             kvt_sb = turn.tile([P, GROUPS, HEAD], F32)
             nc.scalar.copy(out=kvt_sb[:], in_=tr_ps[:])
-            mix_ps = psum.tile([P, GROUPS, HEAD], F32)
+            return kvt_sb
+
+        def mix_slab(psum_t, kvt_sb, c):
+            mix_ps = psum_t.tile([P, GROUPS, HEAD], F32)
             for g in range(GROUPS):
                 nc.tensor.matmul(
                     out=mix_ps[:, g, :],
@@ -151,20 +172,29 @@ def tile_mhla_pa_t_kernel(tc, k_feat, v, w_piece, out):
                 in_=mix_ps[:].rearrange("p g (i y) -> p i g y", y=LANES),
             )
 
-        grouped = regroup(0)
-        for j in range(WINDOWS):
-            following = None
-            if j + 1 < WINDOWS:
-                following = regroup(j + 1)
-            if j + LOADS_AHEAD < WINDOWS:
-                load(j + LOADS_AHEAD)
-            states(grouped, j)
-            if j < WINDOWS - LAST:
-                for i in range(WINDOWS):
-                    vector_mix(i, j)
-            grouped = following
-        for c in range(TENSOR_SLABS):
-            tensor_mix(c)
+        with tc.psum_pool(name="psum_s", bufs=2) as psum_s:
+            grouped = {0: regroup(0), 1: regroup(1)}
+            states(psum_s, grouped[0], 0)
+            gpsimd_mix(0)
+            for j in range(WINDOWS):
+                if j + 2 < WINDOWS:
+                    grouped[j + 2] = regroup(j + 2)
+                if j + LOADS_AHEAD < WINDOWS:
+                    load(j + LOADS_AHEAD)
+                if j + 1 < WINDOWS:
+                    states(psum_s, grouped[j + 1], j + 1)
+                    gpsimd_mix(j + 1)
+                if j < WINDOWS - LAST:
+                    for i in range(WINDOWS):
+                        vector_mix(i, j)
+        with tc.psum_pool(name="psum_t", bufs=2) as psum_t:
+            turned = turn_slab(psum_t, 0)
+            for c in range(TENSOR_SLABS):
+                following = None
+                if c + 1 < TENSOR_SLABS:
+                    following = turn_slab(psum_t, c + 1)
+                mix_slab(psum_t, turned, c)
+                turned = following
         for first in range(0, WINDOWS, CHAINS):
             for j in range(WINDOWS - LAST, WINDOWS):
                 for i in range(first, first + CHAINS):

@@ -83,13 +83,16 @@ def tile_mhla_pa_t_kernel(tc, k_feat, v, w_piece, out):
             grouped = {}
             for name in ("k", "v"):
                 dst = stage.tile([P, GROUPS * HEAD, PACK], BF16, name="grouped_" + name, align_bytes=64)
-                for g in range(GROUPS):
-                    dst_g = dst[:, g * HEAD : (g + 1) * HEAD, :].rearrange("p (c i) t -> p c t i", i=RUN)
-                    src_g = raw[(name, j)][:, g, :, :].rearrange("p t (c i) -> p c t i", i=RUN)
-                    if j == 0:
+                if j == 0:
+                    for g in range(GROUPS):
+                        dst_g = dst[:, g * HEAD : (g + 1) * HEAD, :].rearrange("p (c i) t -> p c t i", i=RUN)
+                        src_g = raw[(name, j)][:, g, :, :].rearrange("p t (c i) -> p c t i", i=RUN)
                         nc.vector.tensor_copy(out=dst_g, in_=src_g)
-                    else:
-                        nc.scalar.copy(out=dst_g, in_=src_g)
+                else:
+                    nc.scalar.copy(
+                        out=dst[:].rearrange("p (g d) t -> p g d t", g=GROUPS),
+                        in_=raw[(name, j)][:].rearrange("p g t d -> p g d t"),
+                    )
                 grouped[name] = dst
             return grouped
 

@@ -16,6 +16,7 @@ GROUPS = 4
 WINDOWS = 16
 HEAD = 128
 RUN = 4
+VECTOR_GROUPS = 1
 LANES = P // WINDOWS
 TENSOR_SLABS = 6
 HALF = HEAD // 2
@@ -83,16 +84,13 @@ def tile_mhla_pa_t_kernel(tc, k_feat, v, w_piece, out):
             grouped = {}
             for name in ("k", "v"):
                 dst = stage.tile([P, GROUPS * HEAD, PACK], BF16, name="grouped_" + name, align_bytes=64)
-                if j == 0:
-                    for g in range(GROUPS):
-                        dst_g = dst[:, g * HEAD : (g + 1) * HEAD, :].rearrange("p (c i) t -> p c t i", i=RUN)
-                        src_g = raw[(name, j)][:, g, :, :].rearrange("p t (c i) -> p c t i", i=RUN)
+                for g in range(GROUPS):
+                    dst_g = dst[:, g * HEAD : (g + 1) * HEAD, :].rearrange("p (c i) t -> p c t i", i=RUN)
+                    src_g = raw[(name, j)][:, g, :, :].rearrange("p t (c i) -> p c t i", i=RUN)
+                    if j == 0 or g < VECTOR_GROUPS:
                         nc.vector.tensor_copy(out=dst_g, in_=src_g)
-                else:
-                    nc.scalar.copy(
-                        out=dst[:].rearrange("p (g d) t -> p g d t", g=GROUPS),
-                        in_=raw[(name, j)][:].rearrange("p g t d -> p g d t"),
-                    )
+                    else:
+                        nc.scalar.copy(out=dst_g, in_=src_g)
                 grouped[name] = dst
             return grouped
 

@@ -16,12 +16,10 @@ GROUPS = 4
 WINDOWS = 16
 HEAD = 128
 RUN = 4
-VECTOR_GROUPS = 1
 LANES = P // WINDOWS
 TENSOR_SLABS = 6
-HALF = HEAD // 2
 TENSOR_COLS = TENSOR_SLABS * LANES
-GPSIMD_COLS = HALF - TENSOR_COLS
+VECTOR_COLS = HEAD - TENSOR_COLS
 LOADS_AHEAD = 6
 CHAINS = 2
 LAST = 4
@@ -39,7 +37,7 @@ def tile_mhla_pa_t_kernel(tc, k_feat, v, w_piece, out):
 
     with tc.tile_pool(name="keep", bufs=1) as keep, tc.tile_pool(name="raw", bufs=LOADS_AHEAD) as raw_pool, tc.tile_pool(
         name="stage", bufs=3
-    ) as stage, tc.tile_pool(name="turn", bufs=2) as turn, tc.psum_pool(name="psum_v", bufs=LAST) as psum_v:
+    ) as stage, tc.tile_pool(name="turn", bufs=2) as turn, tc.psum_pool(name="psum", bufs=2) as psum:
         raw = {}
 
         def load(j):
@@ -76,8 +74,7 @@ def tile_mhla_pa_t_kernel(tc, k_feat, v, w_piece, out):
         )
 
         kv_tensor = keep.tile([P, GROUPS, TENSOR_SLABS, WINDOWS, LANES], F32)
-        kv_gpsimd = keep.tile([P, WINDOWS, GROUPS, GPSIMD_COLS], F32)
-        kv_vector = {}
+        kv_vector = keep.tile([P, WINDOWS, GROUPS, VECTOR_COLS], F32)
         out_sb = keep.tile([P, WINDOWS, GROUPS, HEAD], F32)
 
         def regroup(j):
@@ -87,14 +84,14 @@ def tile_mhla_pa_t_kernel(tc, k_feat, v, w_piece, out):
                 for g in range(GROUPS):
                     dst_g = dst[:, g * HEAD : (g + 1) * HEAD, :].rearrange("p (c i) t -> p c t i", i=RUN)
                     src_g = raw[(name, j)][:, g, :, :].rearrange("p t (c i) -> p c t i", i=RUN)
-                    if j == 0 or g < VECTOR_GROUPS:
+                    if j == 0:
                         nc.vector.tensor_copy(out=dst_g, in_=src_g)
                     else:
                         nc.scalar.copy(out=dst_g, in_=src_g)
                 grouped[name] = dst
             return grouped
 
-        def states(psum_s, grouped, j):
+        def states(grouped, j):
             codes = {}
             scales = {}
             for name in ("k", "v"):
@@ -105,51 +102,35 @@ def tile_mhla_pa_t_kernel(tc, k_feat, v, w_piece, out):
                     scales=scales[name][:],
                     in_=grouped[name][:].rearrange("p c t -> p (c t)"),
                 )
-            low_ps = psum_s.tile([P, GROUPS, HALF], F32)
-            high_ps = psum_v.tile([P, GROUPS, HALF], F32)
-            for half, kv_ps in ((0, low_ps), (1, high_ps)):
-                for g in range(GROUPS):
-                    k_cols = slice(g * HEAD, (g + 1) * HEAD)
-                    v_cols = slice(g * HEAD + half * HALF, g * HEAD + (half + 1) * HALF)
-                    nc.tensor.matmul_mx(
-                        out=kv_ps[:, g, :],
-                        lhsT=codes["k"][:, k_cols].bitcast(FP8X4),
-                        lhsT_scale=scales["k"][:, k_cols],
-                        rhs=codes["v"][:, v_cols].bitcast(FP8X4),
-                        rhs_scale=scales["v"][:, v_cols],
-                        start=True,
-                        stop=True,
-                    )
+            kv_ps = psum.tile([P, GROUPS, HEAD], F32)
+            for g in range(GROUPS):
+                cols = slice(g * HEAD, (g + 1) * HEAD)
+                nc.tensor.matmul_mx(
+                    out=kv_ps[:, g, :],
+                    lhsT=codes["k"][:, cols].bitcast(FP8X4),
+                    lhsT_scale=scales["k"][:, cols],
+                    rhs=codes["v"][:, cols].bitcast(FP8X4),
+                    rhs_scale=scales["v"][:, cols],
+                    start=True,
+                    stop=True,
+                )
             nc.scalar.copy(
                 out=kv_tensor[:, :, :, j, :],
-                in_=low_ps[:, :, 0:TENSOR_COLS].rearrange("p g (c x) -> p g c x", x=LANES),
+                in_=kv_ps[:, :, 0:TENSOR_COLS].rearrange("p g (c x) -> p g c x", x=LANES),
             )
-            nc.scalar.copy(out=kv_gpsimd[:, j, :, :], in_=low_ps[:, :, TENSOR_COLS:HALF])
-            kv_vector[j] = high_ps
-
-        def gpsimd_mix(j):
-            acc = out_sb[:, :, :, TENSOR_COLS:HALF]
-            shape = [P, WINDOWS, GROUPS, GPSIMD_COLS]
-            state = kv_gpsimd[:, j, :, :].unsqueeze(1).to_broadcast(shape)
-            weight = w_all[:, :, j : j + 1].unsqueeze(3).to_broadcast(shape)
-            if j == 0:
-                nc.gpsimd.tensor_tensor(out=acc, in0=state, in1=weight, op=MULT)
-            else:
-                product = turn.tile(shape, F32)
-                nc.gpsimd.tensor_tensor(out=product[:], in0=state, in1=weight, op=MULT)
-                nc.gpsimd.tensor_tensor(out=acc, in0=acc, in1=product[:], op=ADD)
+            nc.scalar.copy(out=kv_vector[:, j, :, :], in_=kv_ps[:, :, TENSOR_COLS:HEAD])
 
         def vector_mix(i, j):
-            acc = out_sb[:, i, :, HALF:HEAD]
+            acc = out_sb[:, i, :, TENSOR_COLS:HEAD]
             if j == 0:
-                nc.vector.tensor_scalar_mul(out=acc, in0=kv_vector[j][:], scalar1=w_all[:, i, j : j + 1])
+                nc.vector.tensor_scalar_mul(out=acc, in0=kv_vector[:, j, :, :], scalar1=w_all[:, i, j : j + 1])
             else:
                 nc.vector.scalar_tensor_tensor(
-                    out=acc, in0=kv_vector[j][:], scalar=w_all[:, i, j : j + 1], in1=acc, op0=MULT, op1=ADD
+                    out=acc, in0=kv_vector[:, j, :, :], scalar=w_all[:, i, j : j + 1], in1=acc, op0=MULT, op1=ADD
                 )
 
-        def turn_slab(psum_t, c):
-            tr_ps = psum_t.tile([P, GROUPS, HEAD], F32)
+        def turn_slab(c):
+            tr_ps = psum.tile([P, GROUPS, HEAD], F32)
             for g in range(GROUPS):
                 nc.tensor.transpose(
                     out=tr_ps[:, g, :], in_=kv_tensor[:, g, c, :, :].rearrange("p j x -> p (j x)"), identity=ident[:]
@@ -158,8 +139,8 @@ def tile_mhla_pa_t_kernel(tc, k_feat, v, w_piece, out):
             nc.scalar.copy(out=kvt_sb[:], in_=tr_ps[:])
             return kvt_sb
 
-        def mix_slab(psum_t, kvt_sb, c):
-            mix_ps = psum_t.tile([P, GROUPS, HEAD], F32)
+        def mix_slab(kvt_sb, c):
+            mix_ps = psum.tile([P, GROUPS, HEAD], F32)
             for g in range(GROUPS):
                 nc.tensor.matmul(
                     out=mix_ps[:, g, :],
@@ -173,29 +154,25 @@ def tile_mhla_pa_t_kernel(tc, k_feat, v, w_piece, out):
                 in_=mix_ps[:].rearrange("p g (i y) -> p i g y", y=LANES),
             )
 
-        with tc.psum_pool(name="psum_s", bufs=2) as psum_s:
-            grouped = {0: regroup(0), 1: regroup(1)}
-            states(psum_s, grouped[0], 0)
-            gpsimd_mix(0)
-            for j in range(WINDOWS):
-                if j + 2 < WINDOWS:
-                    grouped[j + 2] = regroup(j + 2)
-                if j + LOADS_AHEAD < WINDOWS:
-                    load(j + LOADS_AHEAD)
-                if j + 1 < WINDOWS:
-                    states(psum_s, grouped[j + 1], j + 1)
-                    gpsimd_mix(j + 1)
-                if j < WINDOWS - LAST:
-                    for i in range(WINDOWS):
-                        vector_mix(i, j)
-        with tc.psum_pool(name="psum_t", bufs=2) as psum_t:
-            turned = turn_slab(psum_t, 0)
-            for c in range(TENSOR_SLABS):
-                following = None
-                if c + 1 < TENSOR_SLABS:
-                    following = turn_slab(psum_t, c + 1)
-                mix_slab(psum_t, turned, c)
-                turned = following
+        grouped = {0: regroup(0), 1: regroup(1)}
+        states(grouped[0], 0)
+        for j in range(WINDOWS):
+            if j + 2 < WINDOWS:
+                grouped[j + 2] = regroup(j + 2)
+            if j + LOADS_AHEAD < WINDOWS:
+                load(j + LOADS_AHEAD)
+            if j + 1 < WINDOWS:
+                states(grouped[j + 1], j + 1)
+            if j < WINDOWS - LAST:
+                for i in range(WINDOWS):
+                    vector_mix(i, j)
+        turned = turn_slab(0)
+        for c in range(TENSOR_SLABS):
+            following = None
+            if c + 1 < TENSOR_SLABS:
+                following = turn_slab(c + 1)
+            mix_slab(turned, c)
+            turned = following
         for first in range(0, WINDOWS, CHAINS):
             for j in range(WINDOWS - LAST, WINDOWS):
                 for i in range(first, first + CHAINS):

@@ -9,48 +9,245 @@ FP8X4 = mybir.dt.float8_e4m3fn_x4
 MULT = mybir.AluOpType.mult
 ADD = mybir.AluOpType.add
 AXIS_X = mybir.AxisListType.X
+COPY = mybir.ActivationFunctionType.Copy
 
 P = 128
 PACK = 4
-GROUPS = 4
+BATCH = 2
+HEADS = 2
 WINDOWS = 16
 HEAD = 128
 RUN = 4
-LANES = P // WINDOWS
-TENSOR_SLABS = 6
-TENSOR_COLS = TENSOR_SLABS * LANES
-VECTOR_COLS = HEAD - TENSOR_COLS
-LOADS_AHEAD = 6
-CHAINS = 2
-LAST = 4
+LANES = 8
+SLOTS = HEAD // LANES
+KRON_SLOTS = 6
+SUM_SLOTS = SLOTS - KRON_SLOTS
+STEP = 2
+BLOCKS = STEP * HEADS
+UNITS_PER_BATCH = WINDOWS // STEP
+UNITS = BATCH * UNITS_PER_BATCH
+CHUNKS = HEADS * SUM_SLOTS
+BANK_CHUNKS = 4
+BANKS = CHUNKS // BANK_CHUNKS
+RAW_BUFS = 4
+PAIRS = KRON_SLOTS // 2
 
-FLOPS = 2 * GROUPS * WINDOWS * (P * PACK) * HEAD * HEAD + 2 * GROUPS * WINDOWS * WINDOWS * HEAD * HEAD
+FLOPS = 2 * BATCH * HEADS * WINDOWS * (P * PACK) * HEAD * HEAD + 2 * BATCH * HEADS * WINDOWS * WINDOWS * HEAD * HEAD
+
+
+def vector_blocks(unit):
+    if unit == 0:
+        return 5
+    if unit == 1:
+        return 4
+    return 2
+
+
+def scalar_outputs(unit):
+    if unit >= UNITS - 2:
+        return 6
+    return 0
 
 
 def tile_mhla_pa_t_kernel(tc, k_feat, v, w_piece, out):
     nc = tc.nc
     dram_rows = {
-        "k": k_feat.rearrange("b h n (p t) d -> n p (b h) (t d)", t=PACK),
-        "v": v.rearrange("b h n (p t) d -> n p (b h) (t d)", t=PACK),
+        "k": k_feat.rearrange("b h n (p t) d -> b n p h (t d)", t=PACK),
+        "v": v.rearrange("b h n (p t) d -> b n p h (t d)", t=PACK),
     }
-    out_rows = out.rearrange("b h i d e -> i d (b h) e")
+    out_rows = out.rearrange("b h i (y c) e -> b (i y) h (c e)", c=SLOTS)
 
-    with tc.tile_pool(name="keep", bufs=1) as keep, tc.tile_pool(name="raw", bufs=LOADS_AHEAD) as raw_pool, tc.tile_pool(
+    with tc.tile_pool(name="keep", bufs=1) as keep, tc.tile_pool(name="raw", bufs=RAW_BUFS) as raw_pool, tc.tile_pool(
         name="stage", bufs=3
-    ) as stage, tc.tile_pool(name="turn", bufs=2) as turn, tc.psum_pool(name="psum", bufs=2) as psum:
+    ) as stage, tc.tile_pool(name="prod", bufs=4) as prod_pool, tc.tile_pool(name="batch", bufs=2) as batch_pool, tc.psum_pool(
+        name="xps", bufs=2
+    ) as x_pool, tc.psum_pool(name="acc", bufs=1) as acc_pool, tc.manual_schedule():
         raw = {}
+        grouped = {}
+        codes = {}
+        scales = {}
+        x_ps = {}
+        xs = {}
+        xk = {}
+        o_sb = {}
+        acc = {}
+        prod = {}
 
-        def load(j):
+        def load(unit):
+            b, jj = divmod(unit, UNITS_PER_BATCH)
             for name in ("k", "v"):
-                t = raw_pool.tile([P, GROUPS, PACK, HEAD], BF16, name="raw_" + name)
-                nc.sync.dma_start(out=t[:].rearrange("p g t d -> p g (t d)"), in_=dram_rows[name][j])
-                raw[(name, j)] = t
+                raw[(name, unit)] = raw_pool.tile([P, STEP, HEADS, PACK, HEAD], BF16, name="raw_" + name)
+            for n2 in range(STEP):
+                for name in ("k", "v"):
+                    nc.sync.dma_start(
+                        out=raw[(name, unit)][:, n2, :, :, :].rearrange("p h t d -> p h (t d)"),
+                        in_=dram_rows[name][b][jj * STEP + n2],
+                    )
 
         w_bf = keep.tile([P, WINDOWS * WINDOWS], BF16)
         nc.scalar.dma_start(out=w_bf[:], in_=w_piece.rearrange("i j -> (i j)").partition_broadcast(P))
-        for j in range(LOADS_AHEAD):
-            load(j)
+        for unit in range(RAW_BUFS):
+            load(unit)
 
+        def copy(on_vector, dst, src):
+            if on_vector:
+                nc.vector.tensor_copy(out=dst, in_=src)
+            else:
+                nc.scalar.copy(out=dst, in_=src)
+
+        def regroup(unit):
+            for name in ("k", "v"):
+                grouped[(name, unit)] = stage.tile(
+                    [P, BLOCKS * HEAD, PACK], BF16, name="grouped_" + name, align_bytes=64
+                )
+            share = vector_blocks(unit)
+            turn = 0
+            for blk in range(BLOCKS):
+                n2, h = divmod(blk, HEADS)
+                for name in ("k", "v"):
+                    dst = grouped[(name, unit)][:, blk * HEAD : (blk + 1) * HEAD, :].rearrange(
+                        "p (c i) t -> p c t i", i=RUN
+                    )
+                    src = raw[(name, unit)][:, n2, h, :, :].rearrange("p t (c i) -> p c t i", i=RUN)
+                    copy((turn * share) % (2 * BLOCKS) < share, dst, src)
+                    turn += 1
+            if unit + RAW_BUFS < UNITS:
+                load(unit + RAW_BUFS)
+
+        def quantise(unit):
+            for name in ("k", "v"):
+                codes[(name, unit)] = stage.tile([P, BLOCKS * HEAD], U32, name="codes_" + name, align_bytes=64)
+                scales[(name, unit)] = stage.tile([P, BLOCKS * HEAD], U8, name="scales_" + name, align_bytes=64)
+                nc.vector.quantize_mx(
+                    out=codes[(name, unit)][:].bitcast(FP8X4),
+                    scales=scales[(name, unit)][:],
+                    in_=grouped[(name, unit)][:].rearrange("p c t -> p (c t)"),
+                )
+
+        def states(unit):
+            x_ps[unit] = x_pool.tile([P, BLOCKS, HEAD], F32, name="x_ps")
+            for blk in range(BLOCKS):
+                cols = slice(blk * HEAD, (blk + 1) * HEAD)
+                nc.tensor.matmul_mx(
+                    out=x_ps[unit][:, blk, :],
+                    lhsT=codes[("v", unit)][:, cols].bitcast(FP8X4),
+                    lhsT_scale=scales[("v", unit)][:, cols],
+                    rhs=codes[("k", unit)][:, cols].bitcast(FP8X4),
+                    rhs_scale=scales[("k", unit)][:, cols],
+                    start=True,
+                    stop=True,
+                )
+
+        def empty(unit):
+            b, jj = divmod(unit, UNITS_PER_BATCH)
+            if jj == 0:
+                xk[b] = batch_pool.tile([P, HEADS, KRON_SLOTS, WINDOWS, LANES], F32, name="xk")
+            by_slot = x_ps[unit][:].rearrange("p b (y c) -> p b c y", c=SLOTS)
+            xs[unit] = stage.tile([P, BLOCKS, SUM_SLOTS, LANES], F32, name="xs")
+            nc.scalar.copy(out=xs[unit][:], in_=by_slot[:, :, KRON_SLOTS:SLOTS, :])
+            for n2 in range(STEP):
+                nc.scalar.copy(
+                    out=xk[b][:, :, :, jj * STEP + n2, :],
+                    in_=by_slot[:, n2 * HEADS : (n2 + 1) * HEADS, 0:KRON_SLOTS, :],
+                )
+
+        def products(unit, n2):
+            j = (unit % UNITS_PER_BATCH) * STEP + n2
+            prod[(unit, n2)] = prod_pool.tile([P, CHUNKS, WINDOWS, LANES], F32, name="prod")
+            src = xs[unit][:, n2 * HEADS : (n2 + 1) * HEADS, :, :].rearrange("p h q y -> p (h q) y")
+            for i in range(WINDOWS):
+                dst = prod[(unit, n2)][:, :, i, :]
+                if i < WINDOWS - scalar_outputs(unit):
+                    nc.vector.tensor_scalar_mul(out=dst, in0=src, scalar1=w_all[:, i, j : j + 1])
+                else:
+                    nc.scalar.activation(out=dst, in_=src, func=COPY, scale=w_all[:, i, j : j + 1])
+
+        def sums(unit, n2):
+            b, jj = divmod(unit, UNITS_PER_BATCH)
+            j = jj * STEP + n2
+            for ch in range(CHUNKS):
+                bank, place = divmod(ch, BANK_CHUNKS)
+                if j == 0 and place == 0:
+                    acc[(b, bank)] = acc_pool.tile([P, BANK_CHUNKS, HEAD], F32, name="acc%d" % bank)
+                nc.tensor.matmul(
+                    out=acc[(b, bank)][:, place, :],
+                    lhsT=prod[(unit, n2)][:, ch, :, :].rearrange("p i y -> p (i y)"),
+                    rhs=ident[:],
+                    is_transpose=True,
+                    start=(j == 0 and place == 0),
+                    stop=(j == WINDOWS - 1 and place == BANK_CHUNKS - 1),
+                )
+
+        def empty_sums(b, bank, on_vector):
+            first = bank * BANK_CHUNKS
+            while first < (bank + 1) * BANK_CHUNKS:
+                h, q = divmod(first, SUM_SLOTS)
+                count = min((bank + 1) * BANK_CHUNKS - first, SUM_SLOTS - q)
+                place = first - bank * BANK_CHUNKS
+                copy(
+                    on_vector,
+                    o_sb[b][:, h, KRON_SLOTS + q : KRON_SLOTS + q + count, :],
+                    acc[(b, bank)][:, place : place + count, :],
+                )
+                first += count
+
+        def store_sums(b, h):
+            nc.sync.dma_start(
+                out=out_rows[b][:, h, KRON_SLOTS * HEAD : SLOTS * HEAD],
+                in_=o_sb[b][:, h, KRON_SLOTS:SLOTS, :].rearrange("p c e -> p (c e)"),
+            )
+
+        def store_kron(b):
+            nc.sync.dma_start(
+                out=out_rows[b][:, :, 0 : KRON_SLOTS * HEAD],
+                in_=o_sb[b][:, :, 0:KRON_SLOTS, :].rearrange("p h c e -> p h (c e)"),
+            )
+
+        turned_ps = {}
+        turned = {}
+        mixed_ps = {}
+
+        def bank_for(b, pair):
+            if b == BATCH - 1 and pair > 0:
+                return x_pool.tile([P, 2, HEADS, HEAD], F32, name="x_ps")
+            return acc_pool.tile([P, 2, HEADS, HEAD], F32, name="kron_ps")
+
+        def kron_turn(b, pair):
+            turned_ps[(b, pair)] = bank_for(b, pair)
+            for s2 in range(2):
+                for h in range(HEADS):
+                    nc.tensor.transpose(
+                        out=turned_ps[(b, pair)][:, s2, h, :],
+                        in_=xk[b][:, h, pair * 2 + s2, :, :].rearrange("p j x -> p (j x)"),
+                        identity=ident[:],
+                    )
+
+        def kron_turn_out(b, pair, on_vector):
+            turned[(b, pair)] = stage.tile([P, 2, HEADS, HEAD], F32, name="turned")
+            copy(on_vector, turned[(b, pair)][:], turned_ps[(b, pair)][:])
+
+        def kron_mix(b, pair):
+            mixed_ps[(b, pair)] = bank_for(b, pair)
+            for s2 in range(2):
+                nc.tensor.matmul(
+                    out=mixed_ps[(b, pair)][:, s2, :, :].rearrange("p h e -> p (h e)"),
+                    lhsT=w_kron[:].rearrange("p i y -> p (i y)"),
+                    rhs=turned[(b, pair)][:, s2, :, :].rearrange("p h e -> p (h e)"),
+                    start=True,
+                    stop=True,
+                )
+
+        def kron_mix_out(b, pair, on_vector):
+            copy(
+                on_vector,
+                o_sb[b][:, :, pair * 2 : pair * 2 + 2, :].rearrange("p h s e -> p s h e"),
+                mixed_ps[(b, pair)][:],
+            )
+
+        for b in range(BATCH):
+            o_sb[b] = batch_pool.tile([P, HEADS, SLOTS, HEAD], F32, name="o_sb")
+
+        regroup(0)
         w_all = keep.tile([P, WINDOWS, WINDOWS], F32)
         nc.vector.tensor_copy(out=w_all[:].rearrange("p i j -> p (i j)"), in_=w_bf[:])
         ident = keep.tile([P, P], F32)
@@ -72,110 +269,54 @@ def tile_mhla_pa_t_kernel(tc, k_feat, v, w_piece, out):
             in1=own_x[:].unsqueeze(1).to_broadcast([P, WINDOWS, LANES]),
             op=MULT,
         )
-
-        kv_tensor = keep.tile([P, GROUPS, TENSOR_SLABS, WINDOWS, LANES], F32)
-        kv_vector = keep.tile([P, WINDOWS, GROUPS, VECTOR_COLS], F32)
-        out_sb = keep.tile([P, WINDOWS, GROUPS, HEAD], F32)
-
-        def regroup(j):
-            grouped = {}
-            for name in ("k", "v"):
-                dst = stage.tile([P, GROUPS * HEAD, PACK], BF16, name="grouped_" + name, align_bytes=64)
-                for g in range(GROUPS):
-                    dst_g = dst[:, g * HEAD : (g + 1) * HEAD, :].rearrange("p (c i) t -> p c t i", i=RUN)
-                    src_g = raw[(name, j)][:, g, :, :].rearrange("p t (c i) -> p c t i", i=RUN)
-                    if j == 0:
-                        nc.vector.tensor_copy(out=dst_g, in_=src_g)
-                    else:
-                        nc.scalar.copy(out=dst_g, in_=src_g)
-                grouped[name] = dst
-            return grouped
-
-        def states(grouped, j):
-            codes = {}
-            scales = {}
-            for name in ("k", "v"):
-                codes[name] = stage.tile([P, GROUPS * HEAD], U32, name="codes_" + name, align_bytes=64)
-                scales[name] = stage.tile([P, GROUPS * HEAD], U8, name="scales_" + name, align_bytes=64)
-                nc.vector.quantize_mx(
-                    out=codes[name][:].bitcast(FP8X4),
-                    scales=scales[name][:],
-                    in_=grouped[name][:].rearrange("p c t -> p (c t)"),
-                )
-            kv_ps = psum.tile([P, GROUPS, HEAD], F32)
-            for g in range(GROUPS):
-                cols = slice(g * HEAD, (g + 1) * HEAD)
-                nc.tensor.matmul_mx(
-                    out=kv_ps[:, g, :],
-                    lhsT=codes["k"][:, cols].bitcast(FP8X4),
-                    lhsT_scale=scales["k"][:, cols],
-                    rhs=codes["v"][:, cols].bitcast(FP8X4),
-                    rhs_scale=scales["v"][:, cols],
-                    start=True,
-                    stop=True,
-                )
-            nc.scalar.copy(
-                out=kv_tensor[:, :, :, j, :],
-                in_=kv_ps[:, :, 0:TENSOR_COLS].rearrange("p g (c x) -> p g c x", x=LANES),
-            )
-            nc.scalar.copy(out=kv_vector[:, j, :, :], in_=kv_ps[:, :, TENSOR_COLS:HEAD])
-
-        def vector_mix(i, j):
-            acc = out_sb[:, i, :, TENSOR_COLS:HEAD]
-            if j == 0:
-                nc.vector.tensor_scalar_mul(out=acc, in0=kv_vector[:, j, :, :], scalar1=w_all[:, i, j : j + 1])
-            else:
-                nc.vector.scalar_tensor_tensor(
-                    out=acc, in0=kv_vector[:, j, :, :], scalar=w_all[:, i, j : j + 1], in1=acc, op0=MULT, op1=ADD
-                )
-
-        def turn_slab(c):
-            tr_ps = psum.tile([P, GROUPS, HEAD], F32)
-            for g in range(GROUPS):
-                nc.tensor.transpose(
-                    out=tr_ps[:, g, :], in_=kv_tensor[:, g, c, :, :].rearrange("p j x -> p (j x)"), identity=ident[:]
-                )
-            kvt_sb = turn.tile([P, GROUPS, HEAD], F32)
-            nc.scalar.copy(out=kvt_sb[:], in_=tr_ps[:])
-            return kvt_sb
-
-        def mix_slab(kvt_sb, c):
-            mix_ps = psum.tile([P, GROUPS, HEAD], F32)
-            for g in range(GROUPS):
-                nc.tensor.matmul(
-                    out=mix_ps[:, g, :],
-                    lhsT=kvt_sb[:, g, :],
-                    rhs=w_kron[:].rearrange("p i y -> p (i y)"),
-                    start=True,
-                    stop=True,
-                )
-            nc.scalar.copy(
-                out=out_sb[:, :, :, c * LANES : (c + 1) * LANES],
-                in_=mix_ps[:].rearrange("p g (i y) -> p i g y", y=LANES),
-            )
-
-        grouped = {0: regroup(0), 1: regroup(1)}
-        states(grouped[0], 0)
-        for j in range(WINDOWS):
-            if j + 2 < WINDOWS:
-                grouped[j + 2] = regroup(j + 2)
-            if j + LOADS_AHEAD < WINDOWS:
-                load(j + LOADS_AHEAD)
-            if j + 1 < WINDOWS:
-                states(grouped[j + 1], j + 1)
-            if j < WINDOWS - LAST:
-                for i in range(WINDOWS):
-                    vector_mix(i, j)
-        turned = turn_slab(0)
-        for c in range(TENSOR_SLABS):
-            following = None
-            if c + 1 < TENSOR_SLABS:
-                following = turn_slab(c + 1)
-            mix_slab(turned, c)
-            turned = following
-        for first in range(0, WINDOWS, CHAINS):
-            for j in range(WINDOWS - LAST, WINDOWS):
-                for i in range(first, first + CHAINS):
-                    vector_mix(i, j)
-            for i in range(first, first + CHAINS):
-                nc.sync.dma_start(out=out_rows[i], in_=out_sb[:, i, :, :])
+        regroup(1)
+        quantise(0)
+        states(0)
+        empty(0)
+        for unit in range(UNITS):
+            if unit + 2 < UNITS:
+                regroup(unit + 2)
+            if unit + 1 < UNITS:
+                quantise(unit + 1)
+                states(unit + 1)
+            if unit == UNITS_PER_BATCH:
+                for bank in range(BANKS):
+                    empty_sums(0, bank, bank < 2)
+                for h in range(HEADS):
+                    store_sums(0, h)
+            step = unit - UNITS_PER_BATCH
+            if 0 <= step < 2 * PAIRS:
+                if step % 2 == 0:
+                    kron_turn_out(0, step // 2, False)
+                else:
+                    kron_mix_out(0, step // 2, False)
+                if step == 2 * PAIRS - 1:
+                    store_kron(0)
+            if unit + 1 < UNITS:
+                empty(unit + 1)
+            if unit == UNITS - 1:
+                for pair in range(PAIRS):
+                    kron_turn(1, pair)
+            products(unit, 0)
+            if unit == UNITS - 1:
+                for pair in range(PAIRS):
+                    kron_turn_out(1, pair, False)
+            sums(unit, 0)
+            products(unit, 1)
+            sums(unit, 1)
+            step = unit - UNITS_PER_BATCH + 1
+            if 0 <= step < 2 * PAIRS:
+                if step % 2 == 0:
+                    kron_turn(0, step // 2)
+                else:
+                    kron_mix(0, step // 2)
+        for pair in range(PAIRS):
+            kron_mix(1, pair)
+        for bank in range(BANKS):
+            empty_sums(1, bank, bank % 2 == 0)
+            if bank == 2:
+                store_sums(1, 0)
+        store_sums(1, 1)
+        for pair in range(PAIRS):
+            kron_mix_out(1, pair, pair % 2 == 0)
+        store_kron(1)

@@ -35,15 +35,13 @@ PAIRS = KRON_SLOTS // 2
 FLOPS = 2 * BATCH * HEADS * WINDOWS * (P * PACK) * HEAD * HEAD + 2 * BATCH * HEADS * WINDOWS * WINDOWS * HEAD * HEAD
 
 
-def vector_blocks(unit):
-    if unit == 0:
-        return 5
-    if unit == 1:
-        return 4
-    return 2
+def vector_pieces(unit):
+    if unit < 2:
+        return 2
+    return unit % 2
 
 
-def scalar_outputs(unit):
+def scalar_outputs(unit, n2):
     if unit >= UNITS - 2:
         return 6
     return 0
@@ -95,45 +93,41 @@ def tile_mhla_pa_t_kernel(tc, k_feat, v, w_piece, out):
             else:
                 nc.scalar.copy(out=dst, in_=src)
 
-        def regroup(unit):
-            for name in ("k", "v"):
-                grouped[(name, unit)] = stage.tile(
-                    [P, BLOCKS * HEAD, PACK], BF16, name="grouped_" + name, align_bytes=64
+        def regroup(unit, n2):
+            if n2 == 0:
+                grouped[unit] = stage.tile([P, 2 * BLOCKS * HEAD, PACK], BF16, name="grouped", align_bytes=64)
+            share = vector_pieces(unit)
+            for side, name in enumerate(("k", "v")):
+                turn = n2 * 2 + side
+                first = (side * BLOCKS + n2 * HEADS) * HEAD
+                dst = grouped[unit][:, first : first + HEADS * HEAD, :].rearrange(
+                    "p (h c i) t -> p h c t i", h=HEADS, i=RUN
                 )
-            share = vector_blocks(unit)
-            turn = 0
-            for blk in range(BLOCKS):
-                n2, h = divmod(blk, HEADS)
-                for name in ("k", "v"):
-                    dst = grouped[(name, unit)][:, blk * HEAD : (blk + 1) * HEAD, :].rearrange(
-                        "p (c i) t -> p c t i", i=RUN
-                    )
-                    src = raw[(name, unit)][:, n2, h, :, :].rearrange("p t (c i) -> p c t i", i=RUN)
-                    copy((turn * share) % (2 * BLOCKS) < share, dst, src)
-                    turn += 1
-            if unit + RAW_BUFS < UNITS:
+                src = raw[(name, unit)][:, n2, :, :, :].rearrange("p h t (c i) -> p h c t i", i=RUN)
+                copy((turn * share) % (2 * STEP) < share, dst, src)
+            if n2 == STEP - 1 and unit + RAW_BUFS < UNITS:
                 load(unit + RAW_BUFS)
 
         def quantise(unit):
-            for name in ("k", "v"):
-                codes[(name, unit)] = stage.tile([P, BLOCKS * HEAD], U32, name="codes_" + name, align_bytes=64)
-                scales[(name, unit)] = stage.tile([P, BLOCKS * HEAD], U8, name="scales_" + name, align_bytes=64)
-                nc.vector.quantize_mx(
-                    out=codes[(name, unit)][:].bitcast(FP8X4),
-                    scales=scales[(name, unit)][:],
-                    in_=grouped[(name, unit)][:].rearrange("p c t -> p (c t)"),
-                )
+            codes[unit] = stage.tile([P, 2 * BLOCKS * HEAD], U32, name="codes", align_bytes=64)
+            scales[unit] = stage.tile([P, 2 * BLOCKS * HEAD], U8, name="scales", align_bytes=64)
+            nc.vector.quantize_mx(
+                out=codes[unit][:].bitcast(FP8X4),
+                scales=scales[unit][:],
+                in_=grouped[unit][:].rearrange("p c t -> p (c t)"),
+            )
 
         def states(unit):
             x_ps[unit] = x_pool.tile([P, BLOCKS, HEAD], F32, name="x_ps")
             for blk in range(BLOCKS):
-                cols = slice(blk * HEAD, (blk + 1) * HEAD)
+                k_cols = slice(blk * HEAD, (blk + 1) * HEAD)
+                v_cols = slice((BLOCKS + blk) * HEAD, (BLOCKS + blk + 1) * HEAD)
                 nc.tensor.matmul_mx(
                     out=x_ps[unit][:, blk, :],
-                    lhsT=codes[("v", unit)][:, cols].bitcast(FP8X4),
-                    lhsT_scale=scales[("v", unit)][:, cols],
-                    rhs=codes[("k", unit)][:, cols].bitcast(FP8X4),
-                    rhs_scale=scales[("k", unit)][:, cols],
+                    lhsT=codes[unit][:, v_cols].bitcast(FP8X4),
+                    lhsT_scale=scales[unit][:, v_cols],
+                    rhs=codes[unit][:, k_cols].bitcast(FP8X4),
+                    rhs_scale=scales[unit][:, k_cols],
                     start=True,
                     stop=True,
                 )
@@ -145,11 +139,10 @@ def tile_mhla_pa_t_kernel(tc, k_feat, v, w_piece, out):
             by_slot = x_ps[unit][:].rearrange("p b (y c) -> p b c y", c=SLOTS)
             xs[unit] = stage.tile([P, BLOCKS, SUM_SLOTS, LANES], F32, name="xs")
             nc.scalar.copy(out=xs[unit][:], in_=by_slot[:, :, KRON_SLOTS:SLOTS, :])
-            for n2 in range(STEP):
-                nc.scalar.copy(
-                    out=xk[b][:, :, :, jj * STEP + n2, :],
-                    in_=by_slot[:, n2 * HEADS : (n2 + 1) * HEADS, 0:KRON_SLOTS, :],
-                )
+            nc.scalar.copy(
+                out=xk[b][:, :, :, jj * STEP : (jj + 1) * STEP, :].rearrange("p h c n x -> p n h c x"),
+                in_=by_slot[:, :, 0:KRON_SLOTS, :].rearrange("p (n h) c x -> p n h c x", h=HEADS),
+            )
 
         def products(unit, n2):
             j = (unit % UNITS_PER_BATCH) * STEP + n2
@@ -157,7 +150,7 @@ def tile_mhla_pa_t_kernel(tc, k_feat, v, w_piece, out):
             src = xs[unit][:, n2 * HEADS : (n2 + 1) * HEADS, :, :].rearrange("p h q y -> p (h q) y")
             for i in range(WINDOWS):
                 dst = prod[(unit, n2)][:, :, i, :]
-                if i < WINDOWS - scalar_outputs(unit):
+                if i < WINDOWS - scalar_outputs(unit, n2):
                     nc.vector.tensor_scalar_mul(out=dst, in0=src, scalar1=w_all[:, i, j : j + 1])
                 else:
                     nc.scalar.activation(out=dst, in_=src, func=COPY, scale=w_all[:, i, j : j + 1])
@@ -247,7 +240,10 @@ def tile_mhla_pa_t_kernel(tc, k_feat, v, w_piece, out):
         for b in range(BATCH):
             o_sb[b] = batch_pool.tile([P, HEADS, SLOTS, HEAD], F32, name="o_sb")
 
-        regroup(0)
+        regroup(0, 0)
+        regroup(0, 1)
+        quantise(0)
+        states(0)
         w_all = keep.tile([P, WINDOWS, WINDOWS], F32)
         nc.vector.tensor_copy(out=w_all[:].rearrange("p i j -> p (i j)"), in_=w_bf[:])
         ident = keep.tile([P, P], F32)
@@ -269,13 +265,13 @@ def tile_mhla_pa_t_kernel(tc, k_feat, v, w_piece, out):
             in1=own_x[:].unsqueeze(1).to_broadcast([P, WINDOWS, LANES]),
             op=MULT,
         )
-        regroup(1)
-        quantise(0)
-        states(0)
+        regroup(1, 0)
+        regroup(1, 1)
         empty(0)
         for unit in range(UNITS):
             if unit + 2 < UNITS:
-                regroup(unit + 2)
+                regroup(unit + 2, 0)
+                regroup(unit + 2, 1)
             if unit + 1 < UNITS:
                 quantise(unit + 1)
                 states(unit + 1)

@@ -41,10 +41,13 @@ def vector_pieces(unit):
     return unit % 2
 
 
-def scalar_outputs(unit, n2):
-    if unit >= UNITS - 2:
+PAIRED = 2
+
+
+def scalar_outputs(unit):
+    if unit == UNITS - 1:
         return 6
-    return 0
+    return 10
 
 
 def tile_mhla_pa_t_kernel(tc, k_feat, v, w_piece, out):
@@ -150,12 +153,21 @@ def tile_mhla_pa_t_kernel(tc, k_feat, v, w_piece, out):
             src = xs[unit][:, n2 * HEADS : (n2 + 1) * HEADS, :, :].rearrange("p h q y -> p (h q) y")
             for i in range(WINDOWS):
                 dst = prod[(unit, n2)][:, :, i, :]
-                if i < WINDOWS - scalar_outputs(unit, n2):
+                if unit < UNITS - PAIRED or i < WINDOWS - scalar_outputs(unit):
                     nc.vector.tensor_scalar_mul(out=dst, in0=src, scalar1=w_all[:, i, j : j + 1])
                 else:
                     nc.scalar.activation(out=dst, in_=src, func=COPY, scale=w_all[:, i, j : j + 1])
 
-        def sums(unit, n2):
+        def add_second(unit):
+            j = (unit % UNITS_PER_BATCH) * STEP + 1
+            src = xs[unit][:, HEADS : 2 * HEADS, :, :].rearrange("p h q y -> p (h q) y")
+            for i in range(WINDOWS):
+                dst = prod[(unit, 0)][:, :, i, :]
+                nc.vector.scalar_tensor_tensor(
+                    out=dst, in0=src, scalar=w_all[:, i, j : j + 1], in1=dst, op0=MULT, op1=ADD
+                )
+
+        def sums(unit, n2, last):
             b, jj = divmod(unit, UNITS_PER_BATCH)
             j = jj * STEP + n2
             for ch in range(CHUNKS):
@@ -168,7 +180,7 @@ def tile_mhla_pa_t_kernel(tc, k_feat, v, w_piece, out):
                     rhs=ident[:],
                     is_transpose=True,
                     start=(j == 0 and place == 0),
-                    stop=(j == WINDOWS - 1 and place == BANK_CHUNKS - 1),
+                    stop=(last and place == BANK_CHUNKS - 1),
                 )
 
         def empty_sums(b, bank, on_vector):
@@ -181,6 +193,17 @@ def tile_mhla_pa_t_kernel(tc, k_feat, v, w_piece, out):
                     on_vector,
                     o_sb[b][:, h, KRON_SLOTS + q : KRON_SLOTS + q + count, :],
                     acc[(b, bank)][:, place : place + count, :],
+                )
+                first += count
+
+        def store_bank(b, bank):
+            first = bank * BANK_CHUNKS
+            while first < (bank + 1) * BANK_CHUNKS:
+                h, q = divmod(first, SUM_SLOTS)
+                count = min((bank + 1) * BANK_CHUNKS - first, SUM_SLOTS - q)
+                nc.sync.dma_start(
+                    out=out_rows[b][:, h, (KRON_SLOTS + q) * HEAD : (KRON_SLOTS + q + count) * HEAD],
+                    in_=o_sb[b][:, h, KRON_SLOTS + q : KRON_SLOTS + q + count, :].rearrange("p c e -> p (c e)"),
                 )
                 first += count
 
@@ -242,8 +265,6 @@ def tile_mhla_pa_t_kernel(tc, k_feat, v, w_piece, out):
 
         regroup(0, 0)
         regroup(0, 1)
-        quantise(0)
-        states(0)
         w_all = keep.tile([P, WINDOWS, WINDOWS], F32)
         nc.vector.tensor_copy(out=w_all[:].rearrange("p i j -> p (i j)"), in_=w_bf[:])
         ident = keep.tile([P, P], F32)
@@ -265,6 +286,8 @@ def tile_mhla_pa_t_kernel(tc, k_feat, v, w_piece, out):
             in1=own_x[:].unsqueeze(1).to_broadcast([P, WINDOWS, LANES]),
             op=MULT,
         )
+        quantise(0)
+        states(0)
         regroup(1, 0)
         regroup(1, 1)
         empty(0)
@@ -288,31 +311,36 @@ def tile_mhla_pa_t_kernel(tc, k_feat, v, w_piece, out):
                     kron_mix_out(0, step // 2, False)
                 if step == 2 * PAIRS - 1:
                     store_kron(0)
-            if unit + 1 < UNITS:
+            if unit < UNITS - PAIRED:
                 empty(unit + 1)
-            if unit == UNITS - 1:
-                for pair in range(PAIRS):
-                    kron_turn(1, pair)
-            products(unit, 0)
-            if unit == UNITS - 1:
-                for pair in range(PAIRS):
-                    kron_turn_out(1, pair, False)
-            sums(unit, 0)
-            products(unit, 1)
-            sums(unit, 1)
+                products(unit, 0)
+                sums(unit, 0, False)
+                products(unit, 1)
+                sums(unit, 1, unit == UNITS_PER_BATCH - 1)
+            else:
+                products(unit, 0)
+                if unit + 1 < UNITS:
+                    empty(unit + 1)
+                    for pair in range(PAIRS):
+                        kron_turn(1, pair)
+                else:
+                    for pair in range(PAIRS):
+                        kron_mix(1, pair)
+                add_second(unit)
+                if unit + 1 < UNITS:
+                    for pair in range(PAIRS):
+                        kron_turn_out(1, pair, False)
+                else:
+                    for pair in range(PAIRS):
+                        kron_mix_out(1, pair, False)
+                    store_kron(1)
+                sums(unit, 0, unit == UNITS - 1)
             step = unit - UNITS_PER_BATCH + 1
             if 0 <= step < 2 * PAIRS:
                 if step % 2 == 0:
                     kron_turn(0, step // 2)
                 else:
                     kron_mix(0, step // 2)
-        for pair in range(PAIRS):
-            kron_mix(1, pair)
         for bank in range(BANKS):
             empty_sums(1, bank, bank % 2 == 0)
-            if bank == 2:
-                store_sums(1, 0)
-        store_sums(1, 1)
-        for pair in range(PAIRS):
-            kron_mix_out(1, pair, pair % 2 == 0)
-        store_kron(1)
+            store_bank(1, bank)

@@ -38,7 +38,7 @@ FLOPS = 2 * BATCH * HEADS * WINDOWS * (P * PACK) * HEAD * HEAD + 2 * BATCH * HEA
 def vector_pieces(unit):
     if unit < 2:
         return 2
-    return unit % 2
+    return unit % 4 // 3
 
 
 PAIRED = 2

@@ -38,7 +38,7 @@ FLOPS = 2 * BATCH * HEADS * WINDOWS * (P * PACK) * HEAD * HEAD + 2 * BATCH * HEA
 def vector_pieces(unit):
     if unit < 2:
         return 2
-    return unit % 4 // 3
+    return 2 * STEP
 
 
 PAIRED = 2
@@ -47,7 +47,9 @@ PAIRED = 2
 def scalar_outputs(unit):
     if unit == UNITS - 1:
         return 6
-    return 10
+    if unit < UNITS_PER_BATCH or unit == UNITS - 2:
+        return 10
+    return 9
 
 
 def tile_mhla_pa_t_kernel(tc, k_feat, v, w_piece, out):
@@ -147,15 +149,17 @@ def tile_mhla_pa_t_kernel(tc, k_feat, v, w_piece, out):
                 in_=by_slot[:, :, 0:KRON_SLOTS, :].rearrange("p (n h) c x -> p n h c x", h=HEADS),
             )
 
-        def products(unit, n2):
+        def products(unit, n2, on_vector):
             j = (unit % UNITS_PER_BATCH) * STEP + n2
-            prod[(unit, n2)] = prod_pool.tile([P, CHUNKS, WINDOWS, LANES], F32, name="prod")
+            if not on_vector:
+                prod[(unit, n2)] = prod_pool.tile([P, CHUNKS, WINDOWS, LANES], F32, name="prod")
             src = xs[unit][:, n2 * HEADS : (n2 + 1) * HEADS, :, :].rearrange("p h q y -> p (h q) y")
             for i in range(WINDOWS):
                 dst = prod[(unit, n2)][:, :, i, :]
-                if unit < UNITS - PAIRED or i < WINDOWS - scalar_outputs(unit):
-                    nc.vector.tensor_scalar_mul(out=dst, in0=src, scalar1=w_all[:, i, j : j + 1])
-                else:
+                if i < WINDOWS - scalar_outputs(unit):
+                    if on_vector:
+                        nc.vector.tensor_scalar_mul(out=dst, in0=src, scalar1=w_all[:, i, j : j + 1])
+                elif not on_vector:
                     nc.scalar.activation(out=dst, in_=src, func=COPY, scale=w_all[:, i, j : j + 1])
 
         def add_second(unit):
@@ -292,6 +296,9 @@ def tile_mhla_pa_t_kernel(tc, k_feat, v, w_piece, out):
         regroup(1, 1)
         empty(0)
         for unit in range(UNITS):
+            products(unit, 0, False)
+            if unit < UNITS - PAIRED:
+                products(unit, 1, False)
             if unit + 2 < UNITS:
                 regroup(unit + 2, 0)
                 regroup(unit + 2, 1)
@@ -313,12 +320,12 @@ def tile_mhla_pa_t_kernel(tc, k_feat, v, w_piece, out):
                     store_kron(0)
             if unit < UNITS - PAIRED:
                 empty(unit + 1)
-                products(unit, 0)
+                products(unit, 0, True)
                 sums(unit, 0, False)
-                products(unit, 1)
+                products(unit, 1, True)
                 sums(unit, 1, unit == UNITS_PER_BATCH - 1)
             else:
-                products(unit, 0)
+                products(unit, 0, True)
                 if unit + 1 < UNITS:
                     empty(unit + 1)
                     for pair in range(PAIRS):

@@ -78,12 +78,11 @@ def tile_mhla_pa_t_kernel(tc, k_feat, v, w_piece, out):
 
         def load(unit):
             b, jj = divmod(unit, UNITS_PER_BATCH)
-            for name in ("k", "v"):
-                raw[(name, unit)] = raw_pool.tile([P, STEP, HEADS, PACK, HEAD], BF16, name="raw_" + name)
+            raw[unit] = raw_pool.tile([P, 2, STEP, HEADS, PACK, HEAD], BF16, name="raw")
             for n2 in range(STEP):
-                for name in ("k", "v"):
+                for side, name in enumerate(("k", "v")):
                     nc.sync.dma_start(
-                        out=raw[(name, unit)][:, n2, :, :, :].rearrange("p h t d -> p h (t d)"),
+                        out=raw[unit][:, side, n2, :, :, :].rearrange("p h t d -> p h (t d)"),
                         in_=dram_rows[name][b][jj * STEP + n2],
                     )
 
@@ -108,9 +107,18 @@ def tile_mhla_pa_t_kernel(tc, k_feat, v, w_piece, out):
                 dst = grouped[unit][:, first : first + HEADS * HEAD, :].rearrange(
                     "p (h c i) t -> p h c t i", h=HEADS, i=RUN
                 )
-                src = raw[(name, unit)][:, n2, :, :, :].rearrange("p h t (c i) -> p h c t i", i=RUN)
+                src = raw[unit][:, side, n2, :, :, :].rearrange("p h t (c i) -> p h c t i", i=RUN)
                 copy((turn * share) % (2 * STEP) < share, dst, src)
             if n2 == STEP - 1 and unit + RAW_BUFS < UNITS:
+                load(unit + RAW_BUFS)
+
+        def regroup_whole(unit):
+            grouped[unit] = stage.tile([P, 2 * BLOCKS * HEAD, PACK], BF16, name="grouped", align_bytes=64)
+            nc.vector.tensor_copy(
+                out=grouped[unit][:].rearrange("p (b c i) t -> p b c t i", b=2 * BLOCKS, i=RUN),
+                in_=raw[unit][:].rearrange("p s n h t (c i) -> p (s n h) c t i", i=RUN),
+            )
+            if unit + RAW_BUFS < UNITS:
                 load(unit + RAW_BUFS)
 
         def quantise(unit):
@@ -299,9 +307,8 @@ def tile_mhla_pa_t_kernel(tc, k_feat, v, w_piece, out):
             products(unit, 0, False)
             if unit < UNITS - PAIRED:
                 products(unit, 1, False)
-            if unit + 2 < UNITS:
-                regroup(unit + 2, 0)
-                regroup(unit + 2, 1)
+            if 0 < unit and unit + 2 < UNITS:
+                regroup_whole(unit + 2)
             if unit + 1 < UNITS:
                 quantise(unit + 1)
                 states(unit + 1)
@@ -324,6 +331,8 @@ def tile_mhla_pa_t_kernel(tc, k_feat, v, w_piece, out):
                 sums(unit, 0, False)
                 products(unit, 1, True)
                 sums(unit, 1, unit == UNITS_PER_BATCH - 1)
+                if unit == 0:
+                    regroup_whole(2)
             else:
                 products(unit, 0, True)
                 if unit + 1 < UNITS:

@@ -44,12 +44,14 @@ def vector_pieces(unit):
 PAIRED = 2
 
 
-def scalar_outputs(unit):
+def scalar_outputs(unit, n2):
     if unit == UNITS - 1:
         return 6
-    if unit < UNITS_PER_BATCH or unit == UNITS - 2:
+    if unit == UNITS - 2:
         return 10
-    return 9
+    if unit < UNITS_PER_BATCH:
+        return 11 - n2
+    return 10 - n2
 
 
 def tile_mhla_pa_t_kernel(tc, k_feat, v, w_piece, out):
@@ -164,7 +166,7 @@ def tile_mhla_pa_t_kernel(tc, k_feat, v, w_piece, out):
             src = xs[unit][:, n2 * HEADS : (n2 + 1) * HEADS, :, :].rearrange("p h q y -> p (h q) y")
             for i in range(WINDOWS):
                 dst = prod[(unit, n2)][:, :, i, :]
-                if i < WINDOWS - scalar_outputs(unit):
+                if i < WINDOWS - scalar_outputs(unit, n2):
                     if on_vector:
                         nc.vector.tensor_scalar_mul(out=dst, in0=src, scalar1=w_all[:, i, j : j + 1])
                 elif not on_vector:

@@ -29,7 +29,7 @@ UNITS = BATCH * UNITS_PER_BATCH
 CHUNKS = HEADS * SUM_SLOTS
 BANK_CHUNKS = 4
 BANKS = CHUNKS // BANK_CHUNKS
-RAW_BUFS = 4
+RAW_BUFS = 5
 PAIRS = KRON_SLOTS // 2
 
 FLOPS = 2 * BATCH * HEADS * WINDOWS * (P * PACK) * HEAD * HEAD + 2 * BATCH * HEADS * WINDOWS * WINDOWS * HEAD * HEAD
@@ -63,8 +63,8 @@ def tile_mhla_pa_t_kernel(tc, k_feat, v, w_piece, out):
     out_rows = out.rearrange("b h i (y c) e -> b (i y) h (c e)", c=SLOTS)
 
     with tc.tile_pool(name="keep", bufs=1) as keep, tc.tile_pool(name="raw", bufs=RAW_BUFS) as raw_pool, tc.tile_pool(
-        name="stage", bufs=3
-    ) as stage, tc.tile_pool(name="prod", bufs=4) as prod_pool, tc.tile_pool(name="batch", bufs=2) as batch_pool, tc.psum_pool(
+        name="stage", bufs=4
+    ) as stage, tc.tile_pool(name="prod", bufs=6) as prod_pool, tc.tile_pool(name="batch", bufs=2) as batch_pool, tc.psum_pool(
         name="xps", bufs=2
     ) as x_pool, tc.psum_pool(name="acc", bufs=1) as acc_pool, tc.manual_schedule():
         raw = {}

import concourse.mybir as mybir
from concourse.masks import make_identity

F32 = mybir.dt.float32
BF16 = mybir.dt.bfloat16
U32 = mybir.dt.uint32
U8 = mybir.dt.uint8
FP8X4 = mybir.dt.float8_e4m3fn_x4
MULT = mybir.AluOpType.mult
ADD = mybir.AluOpType.add
AXIS_X = mybir.AxisListType.X
COPY = mybir.ActivationFunctionType.Copy

P = 128
PACK = 4
BATCH = 2
HEADS = 2
WINDOWS = 16
HEAD = 128
RUN = 4
LANES = 8
SLOTS = HEAD // LANES
KRON_SLOTS = 6
SUM_SLOTS = SLOTS - KRON_SLOTS
STEP = 2
BLOCKS = STEP * HEADS
UNITS_PER_BATCH = WINDOWS // STEP
UNITS = BATCH * UNITS_PER_BATCH
CHUNKS = HEADS * SUM_SLOTS
BANK_CHUNKS = 4
BANKS = CHUNKS // BANK_CHUNKS
RAW_BUFS = 5
PAIRS = KRON_SLOTS // 2

FLOPS = 2 * BATCH * HEADS * WINDOWS * (P * PACK) * HEAD * HEAD + 2 * BATCH * HEADS * WINDOWS * WINDOWS * HEAD * HEAD


def vector_pieces(unit):
    if unit < 2:
        return 2
    return 2 * STEP


PAIRED = 2


def scalar_outputs(unit, n2):
    if unit == UNITS - 1:
        return 6
    if unit == UNITS - 2:
        return 10
    if unit < UNITS_PER_BATCH:
        return 11 - n2
    return 10 - n2


def tile_mhla_pa_t_kernel(tc, k_feat, v, w_piece, out):
    nc = tc.nc
    dram_rows = {
        "k": k_feat.rearrange("b h n (p t) d -> b n p h (t d)", t=PACK),
        "v": v.rearrange("b h n (p t) d -> b n p h (t d)", t=PACK),
    }
    out_rows = out.rearrange("b h i (y c) e -> b (i y) h (c e)", c=SLOTS)

    with tc.tile_pool(name="keep", bufs=1) as keep, tc.tile_pool(name="raw", bufs=RAW_BUFS) as raw_pool, tc.tile_pool(
        name="stage", bufs=4
    ) as stage, tc.tile_pool(name="prod", bufs=6) as prod_pool, tc.tile_pool(name="batch", bufs=2) as batch_pool, tc.psum_pool(
        name="xps", bufs=2
    ) as x_pool, tc.psum_pool(name="acc", bufs=1) as acc_pool, tc.manual_schedule():
        raw = {}
        grouped = {}
        codes = {}
        scales = {}
        x_ps = {}
        xs = {}
        xk = {}
        o_sb = {}
        acc = {}
        prod = {}

        def load(unit):
            b, jj = divmod(unit, UNITS_PER_BATCH)
            raw[unit] = raw_pool.tile([P, 2, STEP, HEADS, PACK, HEAD], BF16, name="raw")
            for n2 in range(STEP):
                for side, name in enumerate(("k", "v")):
                    nc.sync.dma_start(
                        out=raw[unit][:, side, n2, :, :, :].rearrange("p h t d -> p h (t d)"),
                        in_=dram_rows[name][b][jj * STEP + n2],
                    )

        w_bf = keep.tile([P, WINDOWS * WINDOWS], BF16)
        nc.scalar.dma_start(out=w_bf[:], in_=w_piece.rearrange("i j -> (i j)").partition_broadcast(P))
        for unit in range(RAW_BUFS):
            load(unit)

        def copy(on_vector, dst, src):
            if on_vector:
                nc.vector.tensor_copy(out=dst, in_=src)
            else:
                nc.scalar.copy(out=dst, in_=src)

        def regroup(unit, n2):
            if n2 == 0:
                grouped[unit] = stage.tile([P, 2 * BLOCKS * HEAD, PACK], BF16, name="grouped", align_bytes=64)
            share = vector_pieces(unit)
            for side, name in enumerate(("k", "v")):
                turn = n2 * 2 + side
                first = (side * BLOCKS + n2 * HEADS) * HEAD
                dst = grouped[unit][:, first : first + HEADS * HEAD, :].rearrange(
                    "p (h c i) t -> p h c t i", h=HEADS, i=RUN
                )
                src = raw[unit][:, side, n2, :, :, :].rearrange("p h t (c i) -> p h c t i", i=RUN)
                copy((turn * share) % (2 * STEP) < share, dst, src)
            if n2 == STEP - 1 and unit + RAW_BUFS < UNITS:
                load(unit + RAW_BUFS)

        def regroup_whole(unit):
            grouped[unit] = stage.tile([P, 2 * BLOCKS * HEAD, PACK], BF16, name="grouped", align_bytes=64)
            nc.vector.tensor_copy(
                out=grouped[unit][:].rearrange("p (b c i) t -> p b c t i", b=2 * BLOCKS, i=RUN),
                in_=raw[unit][:].rearrange("p s n h t (c i) -> p (s n h) c t i", i=RUN),
            )
            if unit + RAW_BUFS < UNITS:
                load(unit + RAW_BUFS)

        def quantise(unit):
            codes[unit] = stage.tile([P, 2 * BLOCKS * HEAD], U32, name="codes", align_bytes=64)
            scales[unit] = stage.tile([P, 2 * BLOCKS * HEAD], U8, name="scales", align_bytes=64)
            nc.vector.quantize_mx(
                out=codes[unit][:].bitcast(FP8X4),
                scales=scales[unit][:],
                in_=grouped[unit][:].rearrange("p c t -> p (c t)"),
            )

        def states(unit):
            x_ps[unit] = x_pool.tile([P, BLOCKS, HEAD], F32, name="x_ps")
            for blk in range(BLOCKS):
                k_cols = slice(blk * HEAD, (blk + 1) * HEAD)
                v_cols = slice((BLOCKS + blk) * HEAD, (BLOCKS + blk + 1) * HEAD)
                nc.tensor.matmul_mx(
                    out=x_ps[unit][:, blk, :],
                    lhsT=codes[unit][:, v_cols].bitcast(FP8X4),
                    lhsT_scale=scales[unit][:, v_cols],
                    rhs=codes[unit][:, k_cols].bitcast(FP8X4),
                    rhs_scale=scales[unit][:, k_cols],
                    start=True,
                    stop=True,
                )

        def empty(unit):
            b, jj = divmod(unit, UNITS_PER_BATCH)
            if jj == 0:
                xk[b] = batch_pool.tile([P, HEADS, KRON_SLOTS, WINDOWS, LANES], F32, name="xk")
            by_slot = x_ps[unit][:].rearrange("p b (y c) -> p b c y", c=SLOTS)
            xs[unit] = stage.tile([P, BLOCKS, SUM_SLOTS, LANES], F32, name="xs")
            nc.scalar.copy(out=xs[unit][:], in_=by_slot[:, :, KRON_SLOTS:SLOTS, :])
            nc.scalar.copy(
                out=xk[b][:, :, :, jj * STEP : (jj + 1) * STEP, :].rearrange("p h c n x -> p n h c x"),
                in_=by_slot[:, :, 0:KRON_SLOTS, :].rearrange("p (n h) c x -> p n h c x", h=HEADS),
            )

        def products(unit, n2, on_vector):
            j = (unit % UNITS_PER_BATCH) * STEP + n2
            if not on_vector:
                prod[(unit, n2)] = prod_pool.tile([P, CHUNKS, WINDOWS, LANES], F32, name="prod")
            src = xs[unit][:, n2 * HEADS : (n2 + 1) * HEADS, :, :].rearrange("p h q y -> p (h q) y")
            for i in range(WINDOWS):
                dst = prod[(unit, n2)][:, :, i, :]
                if i < WINDOWS - scalar_outputs(unit, n2):
                    if on_vector:
                        nc.vector.tensor_scalar_mul(out=dst, in0=src, scalar1=w_all[:, i, j : j + 1])
                elif not on_vector:
                    nc.scalar.activation(out=dst, in_=src, func=COPY, scale=w_all[:, i, j : j + 1])

        def add_second(unit):
            j = (unit % UNITS_PER_BATCH) * STEP + 1
            src = xs[unit][:, HEADS : 2 * HEADS, :, :].rearrange("p h q y -> p (h q) y")
            for i in range(WINDOWS):
                dst = prod[(unit, 0)][:, :, i, :]
                nc.vector.scalar_tensor_tensor(
                    out=dst, in0=src, scalar=w_all[:, i, j : j + 1], in1=dst, op0=MULT, op1=ADD
                )

        def sums(unit, n2, last):
            b, jj = divmod(unit, UNITS_PER_BATCH)
            j = jj * STEP + n2
            for ch in range(CHUNKS):
                bank, place = divmod(ch, BANK_CHUNKS)
                if j == 0 and place == 0:
                    acc[(b, bank)] = acc_pool.tile([P, BANK_CHUNKS, HEAD], F32, name="acc%d" % bank)
                nc.tensor.matmul(
                    out=acc[(b, bank)][:, place, :],
                    lhsT=prod[(unit, n2)][:, ch, :, :].rearrange("p i y -> p (i y)"),
                    rhs=ident[:],
                    is_transpose=True,
                    start=(j == 0 and place == 0),
                    stop=(last and place == BANK_CHUNKS - 1),
                )

        def empty_sums(b, bank, on_vector):
            first = bank * BANK_CHUNKS
            while first < (bank + 1) * BANK_CHUNKS:
                h, q = divmod(first, SUM_SLOTS)
                count = min((bank + 1) * BANK_CHUNKS - first, SUM_SLOTS - q)
                place = first - bank * BANK_CHUNKS
                copy(
                    on_vector,
                    o_sb[b][:, h, KRON_SLOTS + q : KRON_SLOTS + q + count, :],
                    acc[(b, bank)][:, place : place + count, :],
                )
                first += count

        def store_bank(b, bank):
            first = bank * BANK_CHUNKS
            while first < (bank + 1) * BANK_CHUNKS:
                h, q = divmod(first, SUM_SLOTS)
                count = min((bank + 1) * BANK_CHUNKS - first, SUM_SLOTS - q)
                nc.sync.dma_start(
                    out=out_rows[b][:, h, (KRON_SLOTS + q) * HEAD : (KRON_SLOTS + q + count) * HEAD],
                    in_=o_sb[b][:, h, KRON_SLOTS + q : KRON_SLOTS + q + count, :].rearrange("p c e -> p (c e)"),
                )
                first += count

        def store_sums(b, h):
            nc.sync.dma_start(
                out=out_rows[b][:, h, KRON_SLOTS * HEAD : SLOTS * HEAD],
                in_=o_sb[b][:, h, KRON_SLOTS:SLOTS, :].rearrange("p c e -> p (c e)"),
            )

        def store_kron(b):
            nc.sync.dma_start(
                out=out_rows[b][:, :, 0 : KRON_SLOTS * HEAD],
                in_=o_sb[b][:, :, 0:KRON_SLOTS, :].rearrange("p h c e -> p h (c e)"),
            )

        turned_ps = {}
        turned = {}
        mixed_ps = {}

        def bank_for(b, pair):
            if b == BATCH - 1 and pair > 0:
                return x_pool.tile([P, 2, HEADS, HEAD], F32, name="x_ps")
            return acc_pool.tile([P, 2, HEADS, HEAD], F32, name="kron_ps")

        def kron_turn(b, pair):
            turned_ps[(b, pair)] = bank_for(b, pair)
            for s2 in range(2):
                for h in range(HEADS):
                    nc.tensor.transpose(
                        out=turned_ps[(b, pair)][:, s2, h, :],
                        in_=xk[b][:, h, pair * 2 + s2, :, :].rearrange("p j x -> p (j x)"),
                        identity=ident[:],
                    )

        def kron_turn_out(b, pair, on_vector):
            turned[(b, pair)] = stage.tile([P, 2, HEADS, HEAD], F32, name="turned")
            copy(on_vector, turned[(b, pair)][:], turned_ps[(b, pair)][:])

        def kron_mix(b, pair):
            mixed_ps[(b, pair)] = bank_for(b, pair)
            for s2 in range(2):
                nc.tensor.matmul(
                    out=mixed_ps[(b, pair)][:, s2, :, :].rearrange("p h e -> p (h e)"),
                    lhsT=w_kron[:].rearrange("p i y -> p (i y)"),
                    rhs=turned[(b, pair)][:, s2, :, :].rearrange("p h e -> p (h e)"),
                    start=True,
                    stop=True,
                )

        def kron_mix_out(b, pair, on_vector):
            copy(
                on_vector,
                o_sb[b][:, :, pair * 2 : pair * 2 + 2, :].rearrange("p h s e -> p s h e"),
                mixed_ps[(b, pair)][:],
            )

        for b in range(BATCH):
            o_sb[b] = batch_pool.tile([P, HEADS, SLOTS, HEAD], F32, name="o_sb")

        regroup(0, 0)
        regroup(0, 1)
        w_all = keep.tile([P, WINDOWS, WINDOWS], F32)
        nc.vector.tensor_copy(out=w_all[:].rearrange("p i j -> p (i j)"), in_=w_bf[:])
        ident = keep.tile([P, P], F32)
        make_identity(nc, ident[:])
        own_j = keep.tile([P, WINDOWS], F32)
        nc.vector.tensor_reduce(out=own_j[:], in_=ident[:].rearrange("p (j x) -> p j x", x=LANES), axis=AXIS_X, op=ADD)
        own_x = keep.tile([P, LANES], F32)
        nc.vector.tensor_reduce(out=own_x[:], in_=ident[:].rearrange("p (j x) -> p x j", x=LANES), axis=AXIS_X, op=ADD)
        picked = keep.tile([P, WINDOWS, WINDOWS], F32)
        nc.vector.tensor_tensor(
            out=picked[:], in0=w_all[:], in1=own_j[:].unsqueeze(1).to_broadcast([P, WINDOWS, WINDOWS]), op=MULT
        )
        w_row = keep.tile([P, WINDOWS], F32)
        nc.vector.tensor_reduce(out=w_row[:], in_=picked[:], axis=AXIS_X, op=ADD)
        w_kron = keep.tile([P, WINDOWS, LANES], F32)
        nc.vector.tensor_tensor(
            out=w_kron[:],
            in0=w_row[:].unsqueeze(2).to_broadcast([P, WINDOWS, LANES]),
            in1=own_x[:].unsqueeze(1).to_broadcast([P, WINDOWS, LANES]),
            op=MULT,
        )
        quantise(0)
        states(0)
        regroup(1, 0)
        regroup(1, 1)
        empty(0)
        for unit in range(UNITS):
            products(unit, 0, False)
            if unit < UNITS - PAIRED:
                products(unit, 1, False)
            if 0 < unit and unit + 2 < UNITS:
                regroup_whole(unit + 2)
            if unit + 1 < UNITS:
                quantise(unit + 1)
                states(unit + 1)
            if unit == UNITS_PER_BATCH:
                for bank in range(BANKS):
                    empty_sums(0, bank, bank < 2)
                for h in range(HEADS):
                    store_sums(0, h)
            step = unit - UNITS_PER_BATCH
            if 0 <= step < 2 * PAIRS:
                if step % 2 == 0:
                    kron_turn_out(0, step // 2, False)
                else:
                    kron_mix_out(0, step // 2, False)
                if step == 2 * PAIRS - 1:
                    store_kron(0)
            if unit < UNITS - PAIRED:
                empty(unit + 1)
                products(unit, 0, True)
                sums(unit, 0, False)
                products(unit, 1, True)
                sums(unit, 1, unit == UNITS_PER_BATCH - 1)
                if unit == 0:
                    regroup_whole(2)
            else:
                products(unit, 0, True)
                if unit + 1 < UNITS:
                    empty(unit + 1)
                    for pair in range(PAIRS):
                        kron_turn(1, pair)
                else:
                    for pair in range(PAIRS):
                        kron_mix(1, pair)
                add_second(unit)
                if unit + 1 < UNITS:
                    for pair in range(PAIRS):
                        kron_turn_out(1, pair, False)
                else:
                    for pair in range(PAIRS):
                        kron_mix_out(1, pair, False)
                    store_kron(1)
                sums(unit, 0, unit == UNITS - 1)
            step = unit - UNITS_PER_BATCH + 1
            if 0 <= step < 2 * PAIRS:
                if step % 2 == 0:
                    kron_turn(0, step // 2)
                else:
                    kron_mix(0, step // 2)
        for bank in range(BANKS):
            empty_sums(1, bank, bank % 2 == 0)
            store_bank(1, bank)
